import numpy as np
import ml_dtypes

BF16 = ml_dtypes.bfloat16


def bf(x):
    return np.asarray(x, np.float32).astype(BF16)


def f32(x):
    return np.asarray(x, np.float32)


def f64(x):
    return np.asarray(x).astype(np.float64)


def striped(idx):
    return np.tile(idx.reshape(-1, 16).T, (8, 1))


D, V, N, B, T, I = 128, 4096, 2048, 4, 512, 4096
EPS = 1e-5
THETA = 160000.0
ERF_TERMS = 150
ERF_LIM = 6.0


def erf(a):
    c = np.clip(a, -ERF_LIM, ERF_LIM)
    a2 = 2.0 * c * c
    term = c.copy()
    tot = c.copy()
    for n in range(1, ERF_TERMS):
        term *= a2
        term /= (2.0 * n + 1.0)
        tot += term
    r = 2.0 / np.sqrt(np.pi) * np.exp(-c * c) * tot
    return np.where(np.abs(a) > ERF_LIM, np.sign(a), r)


def gelu_erf(v):
    return 0.5 * v * (1.0 + erf(v / np.sqrt(2.0)))


def ln(x, gain):
    m = x.mean(0, keepdims=True)
    v = x.var(0, keepdims=True)
    return (x - m) / np.sqrt(v + EPS) * gain


def rot_half(x):
    return np.concatenate([-x[D // 2:], x[:D // 2]], 0)


def rope_tables():
    inv = (np.float32(1.0) / (np.float32(THETA) ** (np.arange(0, D, 2, dtype=np.float32) / np.float32(D)))).astype(np.float32)
    f = (np.arange(T, dtype=np.float32)[:, None] * inv[None, :]).astype(np.float32)
    emb = np.concatenate([f, f], -1).T
    return f32(np.cos(f64(emb))), f32(np.sin(f64(emb)))


def setup_inputs():
    cos, sin = rope_tables()
    return {
        'table': bf(np.random.standard_normal((D, V))),
        'emb_gain': f32(1.0 + 0.1 * np.random.standard_normal((D, 1))),
        'wq': bf(1.3 * np.random.standard_normal((D, D)) / np.sqrt(D)),
        'wk': bf(1.3 * np.random.standard_normal((D, D)) / np.sqrt(D)),
        'wv': bf(np.random.standard_normal((D, D)) / np.sqrt(D)),
        'cos': cos,
        'sin': sin,
        'wo': bf(2.0 * np.random.standard_normal((D, D)) / np.sqrt(D)),
        'mlp_gain': f32(1.0 + 0.1 * np.random.standard_normal((D, 1))),
        'wi_a': f32(np.random.standard_normal((D, I)) / np.sqrt(D)),
        'wi_gate': f32(np.random.standard_normal((D, I)) / np.sqrt(D)),
        'wmo': f32(np.random.standard_normal((I, D)) / np.sqrt(I)),
        'offs': striped(np.random.permutation(np.tile(np.arange(V), 2))[:N]),
    }


def reference(table, emb_gain, wq, wk, wv, cos, sin, wo, mlp_gain, wi_a, wi_gate, wmo, offs):
    idx = offs[:16].T.reshape(-1)
    xn = ln(f64(table), f64(emb_gain))
    x = xn[:, idx]
    q = f64(wq).T @ x
    k = f64(wk).T @ x
    v = f64(wv).T @ x
    cs = np.tile(f64(cos), (1, B))
    sn = np.tile(f64(sin), (1, B))
    qr = q * cs + rot_half(q) * sn
    kr = k * cs + rot_half(k) * sn
    at = np.zeros((D, N))
    for b in range(B):
        sl = slice(b * T, (b + 1) * T)
        sc = qr[:, sl].T @ kr[:, sl] / np.sqrt(D)
        e = np.exp(sc - sc.max(-1, keepdims=True))
        p = e / e.sum(-1, keepdims=True)
        at[:, sl] = v[:, sl] @ p.T
    x1 = x + f64(wo).T @ at
    hm = ln(x1, f64(mlp_gain))
    act = gelu_erf(f64(wi_a).T @ hm) * (f64(wi_gate).T @ hm)
    return x1 + f64(wmo).T @ act

@@ -1,0 +1,246 @@
+import math
+
+import concourse.mybir as mybir
+from concourse.masks import make_identity
+
+F32 = mybir.dt.float32
+BF16 = mybir.dt.bfloat16
+U16 = mybir.dt.uint16
+ALU = mybir.AluOpType
+ACT = mybir.ActivationFunctionType
+AXIS = mybir.AxisListType
+
+D = 128
+V = 4096
+B = 4
+T = 512
+N = B * T
+TB = T // 128
+I = 4096
+IB = I // 128
+EPS = 1e-5
+SCALE = 1.0 / math.sqrt(D)
+
+FLOPS = 2 * D * D * N * 4 + 2 * 2 * D * T * T * B + 3 * 2 * D * I * N
+
+
+def tile_bertrewardmodel_b_kernel(
+    tc, table, emb_gain, wq, wk, wv, cos, sin, wo, mlp_gain, wi_a, wi_gate, wmo, offs, out
+):
+    nc = tc.nc
+    with (
+        tc.tile_pool(name="held", bufs=1) as held,
+        tc.tile_pool(name="ring", bufs=3) as ring,
+        tc.psum_pool(name="psum", bufs=8) as psum,
+    ):
+
+        def bank(dtype, name):
+            return psum.tile([128, T], dtype, name=name, tag="bank")
+
+        offsets = held.tile([128, N // 16], U16, name="offsets")
+        nc.sync.dma_start(offsets[:], offs)
+
+        raw = held.tile([D, V], BF16, name="raw")
+        for c in range(4):
+            cols = slice(c * (V // 4), (c + 1) * (V // 4))
+            queue = nc.sync if c % 2 == 0 else nc.scalar
+            queue.dma_start(raw[:, cols], table[:, cols])
+
+        emb_gain_t = held.tile([D, 1], F32, name="emb_gain_t")
+        nc.scalar.dma_start(emb_gain_t[:], emb_gain)
+        mlp_gain_t = held.tile([D, 1], F32, name="mlp_gain_t")
+        nc.scalar.dma_start(mlp_gain_t[:], mlp_gain)
+        wq_t = held.tile([D, D], BF16, name="wq_t")
+        nc.sync.dma_start(wq_t[:], wq)
+        wk_t = held.tile([D, D], BF16, name="wk_t")
+        nc.scalar.dma_start(wk_t[:], wk)
+        wv_t = held.tile([D, D], BF16, name="wv_t")
+        nc.sync.dma_start(wv_t[:], wv)
+        wo_t = held.tile([D, D], BF16, name="wo_t")
+        nc.scalar.dma_start(wo_t[:], wo)
+        cos_t = held.tile([D, T], F32, name="cos_t")
+        nc.sync.dma_start(cos_t[:], cos)
+        sin_t = held.tile([D, T], F32, name="sin_t")
+        nc.scalar.dma_start(sin_t[:], sin)
+
+        wi_a_f = held.tile([D, I], F32, name="wi_a_f")
+        wi_gate_f = held.tile([D, I], F32, name="wi_gate_f")
+        wmo_f = held.tile([128, IB, D], F32, name="wmo_f")
+        for c in range(4):
+            cols = slice(c * (I // 4), (c + 1) * (I // 4))
+            blocks = slice(c * (IB // 4), (c + 1) * (IB // 4))
+            nc.sync.dma_start(wi_a_f[:, cols], wi_a[:, cols])
+            nc.sync.dma_start(wi_gate_f[:, cols], wi_gate[:, cols])
+            nc.sync.dma_start(wmo_f[:, blocks, :], wmo[cols, :].rearrange("(a p) d -> p a d", p=128))
+
+        ident = held.tile([128, 128], BF16, name="ident")
+        make_identity(nc, ident[:])
+        ident_f = held.tile([128, 128], F32, name="ident_f")
+        make_identity(nc, ident_f[:])
+        centre = held.tile([D, D], BF16, name="centre")
+        nc.vector.tensor_scalar(centre[:], ident[:], -1.0 / D, None, op0=ALU.add)
+        average = held.tile([D, D], BF16, name="average")
+        nc.vector.memset(average[:], 1.0 / D)
+        eps_t = held.tile([128, 1], F32, name="eps_t")
+        nc.vector.memset(eps_t[:], EPS)
+        minus_half = held.tile([128, TB, 1], F32, name="minus_half")
+        nc.vector.memset(minus_half[:], -0.5)
+
+        wq_rot = held.tile([D, D], BF16, name="wq_rot")
+        wk_rot = held.tile([D, D], BF16, name="wk_rot")
+        for rotated, plain in ((wq_rot, wq_t), (wk_rot, wk_t)):
+            nc.vector.tensor_scalar(rotated[:, 0:64], plain[:, 64:128], -1.0, None, op0=ALU.mult)
+            nc.vector.tensor_copy(rotated[:, 64:128], plain[:, 0:64])
+
+        window = held.tile([D, V], BF16, name="window")
+        for c in range(V // T):
+            cols = slice(c * T, (c + 1) * T)
+            centred = bank(F32, "centred")
+            nc.tensor.matmul(centred[:], centre[:], raw[:, cols], start=True, stop=True)
+            squares = ring.tile([D, T], BF16, name="squares")
+            nc.scalar.activation(squares[:], centred[:], ACT.Square)
+            variance = bank(F32, "variance")
+            nc.tensor.matmul(variance[:], average[:], squares[:], start=True, stop=True)
+            rstd = ring.tile([D, T], F32, name="rstd")
+            nc.scalar.activation(rstd[:], variance[:], ACT.Abs_reciprocal_sqrt, bias=eps_t[:])
+            nc.vector.scalar_tensor_tensor(
+                window[:, cols], centred[:], emb_gain_t[:], rstd[:], op0=ALU.mult, op1=ALU.mult
+            )
+
+        q_cos = held.tile([D, N], F32, name="q_cos")
+        k_cos = held.tile([D, N], F32, name="k_cos")
+        v_t = held.tile([D, N], BF16, name="v_t")
+        x_t = held.tile([D, N], BF16, name="x_t")
+        for b in range(B):
+            seq = slice(b * T, (b + 1) * T)
+            looked_up = window[:].indirect(offsets[:, b * (T // 16) : (b + 1) * (T // 16)])
+            q_ps = bank(F32, "q_ps")
+            nc.tensor.matmul(q_ps[:], wq_t[:], looked_up, start=True, stop=True)
+            nc.vector.tensor_tensor(q_cos[:, seq], q_ps[:], cos_t[:], ALU.mult)
+            x_ps = bank(F32, "x_ps")
+            nc.tensor.matmul(x_ps[:], ident[:], looked_up, start=True, stop=True)
+            nc.scalar.copy(x_t[:, seq], x_ps[:])
+            k_ps = bank(F32, "k_ps")
+            nc.tensor.matmul(k_ps[:], wk_t[:], looked_up, start=True, stop=True)
+            nc.vector.tensor_tensor(k_cos[:, seq], k_ps[:], cos_t[:], ALU.mult)
+            v_ps = bank(F32, "v_ps")
+            nc.tensor.matmul(v_ps[:], wv_t[:], looked_up, start=True, stop=True)
+            nc.scalar.copy(v_t[:, seq], v_ps[:])
+
+        qr = held.tile([D, N], BF16, name="qr")
+        kr = held.tile([D, N], BF16, name="kr")
+        v_tok = held.tile([128, N], BF16, name="v_tok")
+        for b in range(B):
+            seq = slice(b * T, (b + 1) * T)
+            for rotated, cos_part, roped in ((wq_rot, q_cos, qr), (wk_rot, k_cos, kr)):
+                rot_ps = bank(F32, "rot_ps")
+                nc.tensor.matmul(rot_ps[:], rotated[:], x_t[:, seq], start=True, stop=True)
+                sin_part = ring.tile([D, T], F32, name="sin_part")
+                nc.vector.tensor_tensor(sin_part[:], rot_ps[:], sin_t[:], ALU.mult)
+                nc.gpsimd.tensor_tensor(roped[:, seq], cos_part[:, seq], sin_part[:], ALU.add)
+            v_tok_ps = bank(BF16, "v_tok_ps")
+            for c in range(TB):
+                nc.tensor.transpose(
+                    v_tok_ps[:, c * 128 : (c + 1) * 128], v_t[:, b * T + c * 128 : b * T + (c + 1) * 128], ident[:]
+                )
+            nc.scalar.copy(v_tok[:, seq], v_tok_ps[:])
+
+        row_max = held.tile([128, B * TB], F32, name="row_max")
+        shift = held.tile([128, B * TB], F32, name="shift")
+        row_sum = held.tile([128, B * TB], F32, name="row_sum")
+        row_inv = held.tile([128, B * TB], F32, name="row_inv")
+        p_key = held.tile([128, B, TB, T], BF16, name="p_key")
+        for b in range(B):
+            seq = slice(b * T, (b + 1) * T)
+            for r in range(TB):
+                n = b * TB + r
+                one = slice(n, n + 1)
+                rows = slice(r * 128, (r + 1) * 128)
+                score = bank(F32, "score")
+                nc.tensor.matmul(
+                    score[:], qr[:, b * T + r * 128 : b * T + (r + 1) * 128], kr[:, seq], start=True, stop=True
+                )
+                nc.vector.tensor_reduce(row_max[:, one], score[:], axis=AXIS.X, op=ALU.max)
+                nc.vector.tensor_scalar(shift[:, one], row_max[:, one], -SCALE, None, op0=ALU.mult)
+                expd = ring.tile([128, T], F32, name="expd")
+                nc.scalar.activation(
+                    expd[:], score[:], ACT.Exp, bias=shift[:, one], scale=SCALE, accum_out=row_sum[:, one]
+                )
+                nc.vector.reciprocal(row_inv[:, one], row_sum[:, one])
+                p_row = ring.tile([128, T], BF16, name="p_row")
+                nc.gpsimd.tensor_scalar(p_row[:], expd[:], row_inv[:, one], 1.0, op0=ALU.mult, op1=ALU.mult)
+                p_key_ps = bank(BF16, "p_key_ps")
+                for c in range(TB):
+                    nc.tensor.transpose(
+                        p_key_ps[:, c * 128 : (c + 1) * 128], p_row[:, c * 128 : (c + 1) * 128], ident[:]
+                    )
+                nc.scalar.copy(p_key[:, b, :, rows], p_key_ps[:].rearrange("u (c j) -> u c j", c=TB))
+
+        at_t = held.tile([D, N], BF16, name="at_t")
+        hm = held.tile([D, N], BF16, name="hm")
+        for b in range(B):
+            seq = slice(b * T, (b + 1) * T)
+            at_ps = bank(F32, "at_ps")
+            for c in range(TB):
+                nc.tensor.matmul(
+                    at_ps[:],
+                    v_tok[:, b * T + c * 128 : b * T + (c + 1) * 128],
+                    p_key[:, b, c, :],
+                    start=(c == 0),
+                    stop=(c == TB - 1),
+                )
+            nc.scalar.copy(at_t[:, seq], at_ps[:])
+
+            x1_tok = bank(F32, "x1_tok")
+            stats = ring.tile([128, TB, 6], F32, name="stats")
+            mean_var = ring.tile([128, TB, 2], F32, name="mean_var")
+            for r in range(TB):
+                rows = slice(r * 128, (r + 1) * 128)
+                tokens = slice(b * T + r * 128, b * T + (r + 1) * 128)
+                nc.tensor.matmul(x1_tok[:, rows], at_t[:, tokens], wo_t[:], start=True, stop=False)
+                nc.tensor.matmul(x1_tok[:, rows], x_t[:, tokens], ident[:], start=False, stop=True)
+                nc.vector.bn_stats(stats[:, r, :], x1_tok[:, rows])
+                nc.vector.bn_aggr(mean_var[:, r, :], stats[:, r, :])
+            var_eps = ring.tile([128, TB, 1], F32, name="var_eps")
+            nc.vector.tensor_scalar(var_eps[:], mean_var[:, :, 1:2], EPS, None, op0=ALU.add)
+            rstd1 = ring.tile([128, TB, 1], F32, name="rstd1")
+            nc.gpsimd.tensor_tensor(rstd1[:], var_eps[:], minus_half[:], ALU.pow)
+            hm_ps = bank(F32, "hm_ps")
+            for r in range(TB):
+                rows = slice(r * 128, (r + 1) * 128)
+                hm_tok = ring.tile([128, D], F32, name="hm_tok", bufs=4)
+                nc.vector.tensor_scalar(
+                    hm_tok[:], x1_tok[:, rows], mean_var[:, r, 0:1], rstd1[:, r, :], op0=ALU.subtract, op1=ALU.mult
+                )
+                nc.tensor.transpose(hm_ps[:, rows], hm_tok[:], ident_f[:])
+            nc.scalar.activation(hm[:, seq], hm_ps[:], ACT.Identity, scale=mlp_gain_t[:])
+
+        wi_a_t = held.tile([D, I], BF16, name="wi_a_t")
+        wi_gate_t = held.tile([D, I], BF16, name="wi_gate_t")
+        wmo_t = held.tile([128, IB, D], BF16, name="wmo_t")
+        for c in range(I // T):
+            cols = slice(c * T, (c + 1) * T)
+            blocks = slice(c * TB, (c + 1) * TB)
+            nc.gpsimd.tensor_scalar(wi_a_t[:, cols], wi_a_f[:, cols], 1.0, 0.0, op0=ALU.mult, op1=ALU.add)
+            nc.gpsimd.tensor_scalar(wi_gate_t[:, cols], wi_gate_f[:, cols], 1.0, 0.0, op0=ALU.mult, op1=ALU.add)
+            nc.gpsimd.tensor_scalar(wmo_t[:, blocks, :], wmo_f[:, blocks, :], 1.0, 0.0, op0=ALU.mult, op1=ALU.add)
+
+        for b in range(B):
+            seq = slice(b * T, (b + 1) * T)
+            out_ps = bank(F32, "out_ps")
+            for a in range(IB):
+                hidden = slice(a * 128, (a + 1) * 128)
+                a_ps = bank(F32, "a_ps")
+                nc.tensor.matmul(a_ps[:], wi_a_t[:, hidden], hm[:, seq], start=True, stop=True)
+                c_ps = bank(F32, "c_ps")
+                nc.tensor.matmul(c_ps[:], wi_gate_t[:, hidden], hm[:, seq], start=True, stop=True)
+                gelu_a = ring.tile([128, T], F32, name="gelu_a", bufs=4)
+                nc.scalar.activation(gelu_a[:], a_ps[:], ACT.Gelu)
+                act = ring.tile([128, T], BF16, name="act", bufs=4)
+                nc.vector.tensor_tensor(act[:], c_ps[:], gelu_a[:], ALU.mult)
+                nc.tensor.matmul(out_ps[:], wmo_t[:, a, :], act[:], start=(a == 0), stop=False)
+            nc.tensor.matmul(out_ps[:], wo_t[:], at_t[:, seq], start=False, stop=False)
+            nc.tensor.matmul(out_ps[:], ident[:], x_t[:, seq], start=False, stop=True)
+            result = ring.tile([D, T], F32, name="result", bufs=2)
+            nc.scalar.copy(result[:], out_ps[:])
+            nc.sync.dma_start(out[:, seq], result[:])

@@ -8,20 +8,25 @@ BF16 = mybir.dt.bfloat16
 U16 = mybir.dt.uint16
 ALU = mybir.AluOpType
 ACT = mybir.ActivationFunctionType
-AXIS = mybir.AxisListType
 
+P = 128
 D = 128
 V = 4096
 B = 4
 T = 512
 N = B * T
-TB = T // 128
+TB = T // P
 I = 4096
-IB = I // 128
+IB = I // P
+PER_COLUMN = 16
+BN_STATS = 6
+BN_AGGR = 2
 EPS = 1e-5
 SCALE = 1.0 / math.sqrt(D)
+QUARTERS = 4
+LAG = 2
 
-FLOPS = 2 * D * D * N * 4 + 2 * 2 * D * T * T * B + 3 * 2 * D * I * N
+FLOPS = 4 * 2 * D * D * N + 2 * 2 * D * T * T * B + 3 * 2 * D * I * N
 
 
 def tile_bertrewardmodel_b_kernel(
@@ -31,216 +36,262 @@ def tile_bertrewardmodel_b_kernel(
     with (
         tc.tile_pool(name="held", bufs=1) as held,
         tc.tile_pool(name="ring", bufs=3) as ring,
-        tc.psum_pool(name="psum", bufs=8) as psum,
+        tc.psum_pool(name="psum", bufs=1) as psum,
     ):
+        bank_bufs = {"ring0": 3, "ring1": 3, "sum": 1, "norm": 1}
 
-        def bank(dtype, name):
-            return psum.tile([128, T], dtype, name=name, tag="bank")
-
-        offsets = held.tile([128, N // 16], U16, name="offsets")
-        nc.sync.dma_start(offsets[:], offs)
-
-        raw = held.tile([D, V], BF16, name="raw")
-        for c in range(4):
-            cols = slice(c * (V // 4), (c + 1) * (V // 4))
-            queue = nc.sync if c % 2 == 0 else nc.scalar
-            queue.dma_start(raw[:, cols], table[:, cols])
+        def bank(dtype, name, tag):
+            return psum.tile([P, T], dtype, name=name, tag=tag, bufs=bank_bufs[tag])
 
         emb_gain_t = held.tile([D, 1], F32, name="emb_gain_t")
-        nc.scalar.dma_start(emb_gain_t[:], emb_gain)
-        mlp_gain_t = held.tile([D, 1], F32, name="mlp_gain_t")
-        nc.scalar.dma_start(mlp_gain_t[:], mlp_gain)
+        nc.sync.dma_start(emb_gain_t[:], emb_gain)
+        raw = held.tile([D, V], BF16, name="raw")
+        for chunk in range(V // T):
+            cols = slice(chunk * T, (chunk + 1) * T)
+            nc.sync.dma_start(raw[:, cols], table[:, cols])
+        offsets = held.tile([P, N // PER_COLUMN], U16, name="offsets")
+        nc.sync.dma_start(offsets[:], offs)
         wq_t = held.tile([D, D], BF16, name="wq_t")
         nc.sync.dma_start(wq_t[:], wq)
         wk_t = held.tile([D, D], BF16, name="wk_t")
-        nc.scalar.dma_start(wk_t[:], wk)
+        nc.sync.dma_start(wk_t[:], wk)
         wv_t = held.tile([D, D], BF16, name="wv_t")
         nc.sync.dma_start(wv_t[:], wv)
-        wo_t = held.tile([D, D], BF16, name="wo_t")
-        nc.scalar.dma_start(wo_t[:], wo)
         cos_t = held.tile([D, T], F32, name="cos_t")
         nc.sync.dma_start(cos_t[:], cos)
         sin_t = held.tile([D, T], F32, name="sin_t")
-        nc.scalar.dma_start(sin_t[:], sin)
-
+        nc.sync.dma_start(sin_t[:], sin)
+        wo_t = held.tile([D, D], BF16, name="wo_t")
+        nc.sync.dma_start(wo_t[:], wo)
+        mlp_gain_t = held.tile([D, 1], F32, name="mlp_gain_t")
+        nc.sync.dma_start(mlp_gain_t[:], mlp_gain)
         wi_a_f = held.tile([D, I], F32, name="wi_a_f")
         wi_gate_f = held.tile([D, I], F32, name="wi_gate_f")
-        wmo_f = held.tile([128, IB, D], F32, name="wmo_f")
-        for c in range(4):
-            cols = slice(c * (I // 4), (c + 1) * (I // 4))
-            blocks = slice(c * (IB // 4), (c + 1) * (IB // 4))
+        wmo_f = held.tile([P, IB, D], F32, name="wmo_f")
+        for quarter in range(QUARTERS):
+            cols = slice(quarter * (I // QUARTERS), (quarter + 1) * (I // QUARTERS))
+            hidden_blocks = slice(quarter * (IB // QUARTERS), (quarter + 1) * (IB // QUARTERS))
             nc.sync.dma_start(wi_a_f[:, cols], wi_a[:, cols])
             nc.sync.dma_start(wi_gate_f[:, cols], wi_gate[:, cols])
-            nc.sync.dma_start(wmo_f[:, blocks, :], wmo[cols, :].rearrange("(a p) d -> p a d", p=128))
+            nc.sync.dma_start(wmo_f[:, hidden_blocks, :], wmo[cols, :].rearrange("(a p) d -> p a d", p=P))
 
-        ident = held.tile([128, 128], BF16, name="ident")
+        ident = held.tile([P, P], BF16, name="ident")
         make_identity(nc, ident[:])
-        ident_f = held.tile([128, 128], F32, name="ident_f")
+        ident_f = held.tile([P, P], F32, name="ident_f")
         make_identity(nc, ident_f[:])
         centre = held.tile([D, D], BF16, name="centre")
         nc.vector.tensor_scalar(centre[:], ident[:], -1.0 / D, None, op0=ALU.add)
-        average = held.tile([D, D], BF16, name="average")
+        average = held.tile([D, D], F32, name="average")
         nc.vector.memset(average[:], 1.0 / D)
-        eps_t = held.tile([128, 1], F32, name="eps_t")
+        eps_t = held.tile([P, 1], F32, name="eps_t")
         nc.vector.memset(eps_t[:], EPS)
-        minus_half = held.tile([128, TB, 1], F32, name="minus_half")
+        minus_half = held.tile([P, TB, 1], F32, name="minus_half")
         nc.vector.memset(minus_half[:], -0.5)
-
         wq_rot = held.tile([D, D], BF16, name="wq_rot")
         wk_rot = held.tile([D, D], BF16, name="wk_rot")
         for rotated, plain in ((wq_rot, wq_t), (wk_rot, wk_t)):
-            nc.vector.tensor_scalar(rotated[:, 0:64], plain[:, 64:128], -1.0, None, op0=ALU.mult)
-            nc.vector.tensor_copy(rotated[:, 64:128], plain[:, 0:64])
+            nc.vector.tensor_scalar(rotated[:, 0 : D // 2], plain[:, D // 2 : D], -1.0, None, op0=ALU.mult)
+            nc.vector.tensor_copy(rotated[:, D // 2 : D], plain[:, 0 : D // 2])
 
         window = held.tile([D, V], BF16, name="window")
-        for c in range(V // T):
-            cols = slice(c * T, (c + 1) * T)
-            centred = bank(F32, "centred")
+        for chunk in range(V // T):
+            cols = slice(chunk * T, (chunk + 1) * T)
+            centred = bank(F32, "centred", "ring0")
             nc.tensor.matmul(centred[:], centre[:], raw[:, cols], start=True, stop=True)
-            squares = ring.tile([D, T], BF16, name="squares")
+            squares = ring.tile([D, T], F32, name="squares")
             nc.scalar.activation(squares[:], centred[:], ACT.Square)
-            variance = bank(F32, "variance")
+            gained = ring.tile([D, T], F32, name="gained", bufs=4)
+            nc.vector.tensor_scalar(gained[:], centred[:], emb_gain_t[:], None, op0=ALU.mult)
+            variance = bank(F32, "variance", "ring1")
             nc.tensor.matmul(variance[:], average[:], squares[:], start=True, stop=True)
             rstd = ring.tile([D, T], F32, name="rstd")
             nc.scalar.activation(rstd[:], variance[:], ACT.Abs_reciprocal_sqrt, bias=eps_t[:])
-            nc.vector.scalar_tensor_tensor(
-                window[:, cols], centred[:], emb_gain_t[:], rstd[:], op0=ALU.mult, op1=ALU.mult
-            )
+            nc.vector.tensor_tensor(window[:, cols], gained[:], rstd[:], ALU.mult)
 
         q_cos = held.tile([D, N], F32, name="q_cos")
         k_cos = held.tile([D, N], F32, name="k_cos")
         v_t = held.tile([D, N], BF16, name="v_t")
         x_t = held.tile([D, N], BF16, name="x_t")
+        looked_up = [
+            window[:].indirect(offsets[:, b * (T // PER_COLUMN) : (b + 1) * (T // PER_COLUMN)]) for b in range(B)
+        ]
         for b in range(B):
             seq = slice(b * T, (b + 1) * T)
-            looked_up = window[:].indirect(offsets[:, b * (T // 16) : (b + 1) * (T // 16)])
-            q_ps = bank(F32, "q_ps")
-            nc.tensor.matmul(q_ps[:], wq_t[:], looked_up, start=True, stop=True)
+            q_ps = bank(F32, "q_ps", "ring0")
+            nc.tensor.matmul(q_ps[:], wq_t[:], looked_up[b], start=True, stop=True)
             nc.vector.tensor_tensor(q_cos[:, seq], q_ps[:], cos_t[:], ALU.mult)
-            x_ps = bank(F32, "x_ps")
-            nc.tensor.matmul(x_ps[:], ident[:], looked_up, start=True, stop=True)
-            nc.scalar.copy(x_t[:, seq], x_ps[:])
-            k_ps = bank(F32, "k_ps")
-            nc.tensor.matmul(k_ps[:], wk_t[:], looked_up, start=True, stop=True)
+            k_ps = bank(F32, "k_ps", "ring1")
+            nc.tensor.matmul(k_ps[:], wk_t[:], looked_up[b], start=True, stop=True)
             nc.vector.tensor_tensor(k_cos[:, seq], k_ps[:], cos_t[:], ALU.mult)
-            v_ps = bank(F32, "v_ps")
-            nc.tensor.matmul(v_ps[:], wv_t[:], looked_up, start=True, stop=True)
+            v_ps = bank(F32, "v_ps", "ring0")
+            nc.tensor.matmul(v_ps[:], wv_t[:], looked_up[b], start=True, stop=True)
             nc.scalar.copy(v_t[:, seq], v_ps[:])
+        for b in range(B):
+            x_ps = bank(F32, "x_ps", "ring1")
+            nc.tensor.matmul(x_ps[:], ident[:], looked_up[b], start=True, stop=True)
+            nc.scalar.copy(x_t[:, b * T : (b + 1) * T], x_ps[:])
 
         qr = held.tile([D, N], BF16, name="qr")
         kr = held.tile([D, N], BF16, name="kr")
-        v_tok = held.tile([128, N], BF16, name="v_tok")
+        v_tok = held.tile([P, N], BF16, name="v_tok")
+        x_tok = held.tile([P, N], BF16, name="x_tok")
         for b in range(B):
             seq = slice(b * T, (b + 1) * T)
             for rotated, cos_part, roped in ((wq_rot, q_cos, qr), (wk_rot, k_cos, kr)):
-                rot_ps = bank(F32, "rot_ps")
+                rot_ps = bank(F32, "rot_ps", "ring1")
                 nc.tensor.matmul(rot_ps[:], rotated[:], x_t[:, seq], start=True, stop=True)
                 sin_part = ring.tile([D, T], F32, name="sin_part")
                 nc.vector.tensor_tensor(sin_part[:], rot_ps[:], sin_t[:], ALU.mult)
                 nc.gpsimd.tensor_tensor(roped[:, seq], cos_part[:, seq], sin_part[:], ALU.add)
-            v_tok_ps = bank(BF16, "v_tok_ps")
-            for c in range(TB):
-                nc.tensor.transpose(
-                    v_tok_ps[:, c * 128 : (c + 1) * 128], v_t[:, b * T + c * 128 : b * T + (c + 1) * 128], ident[:]
-                )
-            nc.scalar.copy(v_tok[:, seq], v_tok_ps[:])
-
-        row_max = held.tile([128, B * TB], F32, name="row_max")
-        shift = held.tile([128, B * TB], F32, name="shift")
-        row_sum = held.tile([128, B * TB], F32, name="row_sum")
-        row_inv = held.tile([128, B * TB], F32, name="row_inv")
-        p_key = held.tile([128, B, TB, T], BF16, name="p_key")
-        for b in range(B):
-            seq = slice(b * T, (b + 1) * T)
-            for r in range(TB):
-                n = b * TB + r
-                one = slice(n, n + 1)
-                rows = slice(r * 128, (r + 1) * 128)
-                score = bank(F32, "score")
-                nc.tensor.matmul(
-                    score[:], qr[:, b * T + r * 128 : b * T + (r + 1) * 128], kr[:, seq], start=True, stop=True
-                )
-                nc.vector.tensor_reduce(row_max[:, one], score[:], axis=AXIS.X, op=ALU.max)
-                nc.vector.tensor_scalar(shift[:, one], row_max[:, one], -SCALE, None, op0=ALU.mult)
-                expd = ring.tile([128, T], F32, name="expd")
-                nc.scalar.activation(
-                    expd[:], score[:], ACT.Exp, bias=shift[:, one], scale=SCALE, accum_out=row_sum[:, one]
-                )
-                nc.vector.reciprocal(row_inv[:, one], row_sum[:, one])
-                p_row = ring.tile([128, T], BF16, name="p_row")
-                nc.gpsimd.tensor_scalar(p_row[:], expd[:], row_inv[:, one], 1.0, op0=ALU.mult, op1=ALU.mult)
-                p_key_ps = bank(BF16, "p_key_ps")
-                for c in range(TB):
+            for features_first, tokens_first in ((v_t, v_tok), (x_t, x_tok)):
+                turned_ps = bank(BF16, "turned_ps", "ring1")
+                for kb in range(TB):
                     nc.tensor.transpose(
-                        p_key_ps[:, c * 128 : (c + 1) * 128], p_row[:, c * 128 : (c + 1) * 128], ident[:]
+                        turned_ps[:, kb * P : (kb + 1) * P],
+                        features_first[:, b * T + kb * P : b * T + (kb + 1) * P],
+                        ident[:],
                     )
-                nc.scalar.copy(p_key[:, b, :, rows], p_key_ps[:].rearrange("u (c j) -> u c j", c=TB))
+                nc.scalar.copy(tokens_first[:, seq], turned_ps[:])
 
+        neg_max = held.tile([P, B * TB], F32, name="neg_max")
+        row_sum = held.tile([P, B * TB], F32, name="row_sum")
+        row_inv = held.tile([P, B * TB], F32, name="row_inv")
+        e_key = held.tile([P, B, TB, T], BF16, name="e_key")
         at_t = held.tile([D, N], BF16, name="at_t")
         hm = held.tile([D, N], BF16, name="hm")
+        x1_t = held.tile([D, N], F32, name="x1_t")
         for b in range(B):
             seq = slice(b * T, (b + 1) * T)
-            at_ps = bank(F32, "at_ps")
-            for c in range(TB):
+            for qb in range(TB):
+                n = b * TB + qb
+                score = bank(F32, "score", "ring0")
+                nc.tensor.matmul(score[:], qr[:, n * P : (n + 1) * P], kr[:, seq], start=True, stop=True)
+                neg_score = ring.tile([P, T], F32, name="neg_score", bufs=4)
+                nc.vector.tensor_scalar(
+                    neg_score[:], score[:], -SCALE, None, op0=ALU.mult, op1=ALU.min, accum_out=neg_max[:, n : n + 1]
+                )
+                e_row = ring.tile([P, T], BF16, name="e_row", bufs=4)
+                nc.scalar.activation(
+                    e_row[:],
+                    neg_score[:],
+                    ACT.Exp,
+                    bias=neg_max[:, n : n + 1],
+                    scale=-1.0,
+                    accum_out=row_sum[:, n : n + 1],
+                )
+                e_key_ps = bank(BF16, "e_key_ps", "ring1")
+                for kb in range(TB):
+                    nc.tensor.transpose(e_key_ps[:, kb * P : (kb + 1) * P], e_row[:, kb * P : (kb + 1) * P], ident[:])
+                turned = e_key_ps[:].rearrange("u (kb j) -> u kb j", kb=TB)
+                if qb % 2 == 0:
+                    nc.scalar.copy(e_key[:, b, :, qb * P : (qb + 1) * P], turned)
+                else:
+                    nc.vector.tensor_copy(e_key[:, b, :, qb * P : (qb + 1) * P], turned)
+
+            at_ps = bank(F32, "at_ps", "sum")
+            for kb in range(TB):
                 nc.tensor.matmul(
                     at_ps[:],
-                    v_tok[:, b * T + c * 128 : b * T + (c + 1) * 128],
-                    p_key[:, b, c, :],
-                    start=(c == 0),
-                    stop=(c == TB - 1),
+                    v_tok[:, b * T + kb * P : b * T + (kb + 1) * P],
+                    e_key[:, b, kb, :],
+                    start=(kb == 0),
+                    stop=(kb == TB - 1),
                 )
             nc.scalar.copy(at_t[:, seq], at_ps[:])
 
-            x1_tok = bank(F32, "x1_tok")
-            stats = ring.tile([128, TB, 6], F32, name="stats")
-            mean_var = ring.tile([128, TB, 2], F32, name="mean_var")
-            for r in range(TB):
-                rows = slice(r * 128, (r + 1) * 128)
-                tokens = slice(b * T + r * 128, b * T + (r + 1) * 128)
-                nc.tensor.matmul(x1_tok[:, rows], at_t[:, tokens], wo_t[:], start=True, stop=False)
-                nc.tensor.matmul(x1_tok[:, rows], x_t[:, tokens], ident[:], start=False, stop=True)
-                nc.vector.bn_stats(stats[:, r, :], x1_tok[:, rows])
-                nc.vector.bn_aggr(mean_var[:, r, :], stats[:, r, :])
-            var_eps = ring.tile([128, TB, 1], F32, name="var_eps")
-            nc.vector.tensor_scalar(var_eps[:], mean_var[:, :, 1:2], EPS, None, op0=ALU.add)
-            rstd1 = ring.tile([128, TB, 1], F32, name="rstd1")
-            nc.gpsimd.tensor_tensor(rstd1[:], var_eps[:], minus_half[:], ALU.pow)
-            hm_ps = bank(F32, "hm_ps")
-            for r in range(TB):
-                rows = slice(r * 128, (r + 1) * 128)
-                hm_tok = ring.tile([128, D], F32, name="hm_tok", bufs=4)
-                nc.vector.tensor_scalar(
-                    hm_tok[:], x1_tok[:, rows], mean_var[:, r, 0:1], rstd1[:, r, :], op0=ALU.subtract, op1=ALU.mult
+            proj_ps = bank(F32, "proj_ps", "norm")
+            for qb in range(TB):
+                n = b * TB + qb
+                nc.tensor.matmul(
+                    proj_ps[:, qb * P : (qb + 1) * P], at_t[:, n * P : (n + 1) * P], wo_t[:], start=True, stop=True
                 )
-                nc.tensor.transpose(hm_ps[:, rows], hm_tok[:], ident_f[:])
+            nc.vector.reciprocal(row_inv[:, b * TB : (b + 1) * TB], row_sum[:, b * TB : (b + 1) * TB])
+            x1_tok = ring.tile([P, T], F32, name="x1_tok", bufs=2)
+            stats = ring.tile([P, TB, BN_STATS], F32, name="stats")
+            mean_var = ring.tile([P, TB, BN_AGGR], F32, name="mean_var")
+            for qb in range(TB):
+                n = b * TB + qb
+                feats = slice(qb * P, (qb + 1) * P)
+                nc.vector.scalar_tensor_tensor(
+                    x1_tok[:, feats],
+                    proj_ps[:, feats],
+                    row_inv[:, n : n + 1],
+                    x_tok[:, n * P : (n + 1) * P],
+                    op0=ALU.mult,
+                    op1=ALU.add,
+                )
+                nc.vector.bn_stats(stats[:, qb, :], x1_tok[:, feats])
+                nc.vector.bn_aggr(mean_var[:, qb, :], stats[:, qb, :])
+            var_eps = ring.tile([P, TB, 1], F32, name="var_eps")
+            nc.vector.tensor_scalar(var_eps[:], mean_var[:, :, 1:2], EPS, None, op0=ALU.add)
+            rstd1 = ring.tile([P, TB, 1], F32, name="rstd1")
+            nc.gpsimd.tensor_tensor(rstd1[:], var_eps[:], minus_half[:], ALU.pow)
+
+            hm_ps = bank(F32, "hm_ps", "norm")
+            for qb in range(TB):
+                feats = slice(qb * P, (qb + 1) * P)
+                hm_tok = ring.tile([P, D], F32, name="hm_tok", bufs=4)
+                nc.vector.tensor_scalar(
+                    hm_tok[:], x1_tok[:, feats], mean_var[:, qb, 0:1], rstd1[:, qb, :], op0=ALU.subtract, op1=ALU.mult
+                )
+                nc.tensor.transpose(hm_ps[:, feats], hm_tok[:], ident_f[:])
             nc.scalar.activation(hm[:, seq], hm_ps[:], ACT.Identity, scale=mlp_gain_t[:])
+
+            x1_ps = bank(F32, "x1_ps", "norm")
+            for qb in range(TB):
+                feats = slice(qb * P, (qb + 1) * P)
+                nc.tensor.transpose(x1_ps[:, feats], x1_tok[:, feats], ident_f[:])
+            nc.scalar.copy(x1_t[:, seq], x1_ps[:])
 
         wi_a_t = held.tile([D, I], BF16, name="wi_a_t")
         wi_gate_t = held.tile([D, I], BF16, name="wi_gate_t")
-        wmo_t = held.tile([128, IB, D], BF16, name="wmo_t")
-        for c in range(I // T):
-            cols = slice(c * T, (c + 1) * T)
-            blocks = slice(c * TB, (c + 1) * TB)
+        wmo_t = held.tile([P, IB, D], BF16, name="wmo_t")
+        for part in range(I // T):
+            cols = slice(part * T, (part + 1) * T)
+            hidden_blocks = slice(part * TB, (part + 1) * TB)
             nc.gpsimd.tensor_scalar(wi_a_t[:, cols], wi_a_f[:, cols], 1.0, 0.0, op0=ALU.mult, op1=ALU.add)
             nc.gpsimd.tensor_scalar(wi_gate_t[:, cols], wi_gate_f[:, cols], 1.0, 0.0, op0=ALU.mult, op1=ALU.add)
-            nc.gpsimd.tensor_scalar(wmo_t[:, blocks, :], wmo_f[:, blocks, :], 1.0, 0.0, op0=ALU.mult, op1=ALU.add)
+            nc.gpsimd.tensor_scalar(
+                wmo_t[:, hidden_blocks, :], wmo_f[:, hidden_blocks, :], 1.0, 0.0, op0=ALU.mult, op1=ALU.add
+            )
 
-        for b in range(B):
-            seq = slice(b * T, (b + 1) * T)
-            out_ps = bank(F32, "out_ps")
-            for a in range(IB):
-                hidden = slice(a * 128, (a + 1) * 128)
-                a_ps = bank(F32, "a_ps")
-                nc.tensor.matmul(a_ps[:], wi_a_t[:, hidden], hm[:, seq], start=True, stop=True)
-                c_ps = bank(F32, "c_ps")
-                nc.tensor.matmul(c_ps[:], wi_gate_t[:, hidden], hm[:, seq], start=True, stop=True)
-                gelu_a = ring.tile([128, T], F32, name="gelu_a", bufs=4)
-                nc.scalar.activation(gelu_a[:], a_ps[:], ACT.Gelu)
-                act = ring.tile([128, T], BF16, name="act", bufs=4)
-                nc.vector.tensor_tensor(act[:], c_ps[:], gelu_a[:], ALU.mult)
-                nc.tensor.matmul(out_ps[:], wmo_t[:, a, :], act[:], start=(a == 0), stop=False)
-            nc.tensor.matmul(out_ps[:], wo_t[:], at_t[:, seq], start=False, stop=False)
-            nc.tensor.matmul(out_ps[:], ident[:], x_t[:, seq], start=False, stop=True)
-            result = ring.tile([D, T], F32, name="result", bufs=2)
-            nc.scalar.copy(result[:], out_ps[:])
-            nc.sync.dma_start(out[:, seq], result[:])
+        def gelu_branch(b, a):
+            a_ps = bank(F32, "a_ps", "ring1")
+            nc.tensor.matmul(a_ps[:], wi_a_t[:, a * P : (a + 1) * P], hm[:, b * T : (b + 1) * T], start=True, stop=True)
+            gelu_a = ring.tile([P, T], F32, name="gelu_a", bufs=4)
+            nc.scalar.activation(gelu_a[:], a_ps[:], ACT.Gelu)
+            return gelu_a
+
+        def gate_branch(b, a, gelu_a):
+            c_ps = bank(F32, "c_ps", "ring0")
+            nc.tensor.matmul(
+                c_ps[:], wi_gate_t[:, a * P : (a + 1) * P], hm[:, b * T : (b + 1) * T], start=True, stop=True
+            )
+            act = ring.tile([P, T], BF16, name="act", bufs=LAG + 4)
+            nc.vector.tensor_tensor(act[:], c_ps[:], gelu_a[:], ALU.mult)
+            return act
+
+        def down(b, a, act, out_ps):
+            nc.tensor.matmul(out_ps[:], wmo_t[:, a, :], act[:], start=(a == 0), stop=(a == IB - 1))
+            if a == IB - 1:
+                seq = slice(b * T, (b + 1) * T)
+                result = ring.tile([D, T], F32, name="result", bufs=2)
+                nc.vector.tensor_tensor(result[:], out_ps[:], x1_t[:, seq], ALU.add)
+                nc.sync.dma_start(out[:, seq], result[:])
+
+        work = [(b, a) for b in range(B) for a in range(IB)]
+        acts = []
+        out_banks = []
+        gelu_ahead = gelu_branch(0, 0)
+        for step in range(len(work) + LAG):
+            if step < len(work):
+                b, a = work[step]
+                gelu_a = gelu_ahead
+                if step + 1 < len(work):
+                    gelu_ahead = gelu_branch(work[step + 1][0], work[step + 1][1])
+                acts.append(gate_branch(b, a, gelu_a))
+            if step >= LAG:
+                b, a = work[step - LAG]
+                if a == 0:
+                    out_banks.append(bank(F32, "out_ps", "sum" if b % 2 == 0 else "norm"))
+                down(b, a, acts[step - LAG], out_banks[b])

@@ -38,7 +38,7 @@ def tile_bertrewardmodel_b_kernel(
         tc.tile_pool(name="ring", bufs=3) as ring,
         tc.psum_pool(name="psum", bufs=1) as psum,
     ):
-        bank_bufs = {"ring0": 3, "ring1": 3, "sum": 1, "norm": 1}
+        bank_bufs = {"ring0": 3, "ring1": 3, "chain": 1, "out": 1}
 
         def bank(dtype, name, tag):
             return psum.tile([P, T], dtype, name=name, tag=tag, bufs=bank_bufs[tag])
@@ -135,16 +135,86 @@ def tile_bertrewardmodel_b_kernel(
         kr = held.tile([D, N], BF16, name="kr")
         v_tok = held.tile([P, N], BF16, name="v_tok")
         x_tok = held.tile([P, N], BF16, name="x_tok")
-        for b in range(B):
+        neg_max = held.tile([P, B * TB], F32, name="neg_max")
+        row_sum = held.tile([P, B * TB], F32, name="row_sum")
+        row_inv = held.tile([P, B * TB], F32, name="row_inv")
+        e_key = held.tile([P, B, TB, T], BF16, name="e_key")
+        at_t = held.tile([D, N], BF16, name="at_t")
+        hm = held.tile([D, N], BF16, name="hm")
+        x1_t = held.tile([D, N], F32, name="x1_t")
+
+        def rope_stages(b, rotated, cos_part, roped):
             seq = slice(b * T, (b + 1) * T)
-            for rotated, cos_part, roped in ((wq_rot, q_cos, qr), (wk_rot, k_cos, kr)):
-                rot_ps = bank(F32, "rot_ps", "ring1")
-                nc.tensor.matmul(rot_ps[:], rotated[:], x_t[:, seq], start=True, stop=True)
-                sin_part = ring.tile([D, T], F32, name="sin_part")
-                nc.vector.tensor_tensor(sin_part[:], rot_ps[:], sin_t[:], ALU.mult)
-                nc.gpsimd.tensor_tensor(roped[:, seq], cos_part[:, seq], sin_part[:], ALU.add)
-            for features_first, tokens_first in ((v_t, v_tok), (x_t, x_tok)):
-                turned_ps = bank(BF16, "turned_ps", "ring1")
+            live = {}
+
+            def rotate():
+                live["rot_ps"] = bank(F32, "rot_ps", "ring1")
+                nc.tensor.matmul(live["rot_ps"][:], rotated[:], x_t[:, seq], start=True, stop=True)
+
+            def times_sin():
+                live["sin_part"] = ring.tile([D, T], F32, name="sin_part")
+                nc.vector.tensor_tensor(live["sin_part"][:], live["rot_ps"][:], sin_t[:], ALU.mult)
+
+            def add_parts():
+                nc.gpsimd.tensor_tensor(roped[:, seq], cos_part[:, seq], live["sin_part"][:], ALU.add)
+
+            return [rotate, times_sin, add_parts]
+
+        def softmax_stages(n):
+            b, qb = divmod(n, TB)
+            live = {}
+
+            def scores():
+                live["score"] = bank(F32, "score", "ring0")
+                nc.tensor.matmul(
+                    live["score"][:], qr[:, n * P : (n + 1) * P], kr[:, b * T : (b + 1) * T], start=True, stop=True
+                )
+
+            def maximum():
+                live["neg_score"] = ring.tile([P, T], F32, name="neg_score", bufs=4)
+                nc.vector.tensor_scalar(
+                    live["neg_score"][:],
+                    live["score"][:],
+                    -SCALE,
+                    None,
+                    op0=ALU.mult,
+                    op1=ALU.min,
+                    accum_out=neg_max[:, n : n + 1],
+                )
+
+            def exponential():
+                live["e_row"] = ring.tile([P, T], BF16, name="e_row", bufs=4)
+                nc.scalar.activation(
+                    live["e_row"][:],
+                    live["neg_score"][:],
+                    ACT.Exp,
+                    bias=neg_max[:, n : n + 1],
+                    scale=-1.0,
+                    accum_out=row_sum[:, n : n + 1],
+                )
+
+            def turn_keys():
+                live["e_key_ps"] = bank(BF16, "e_key_ps", "ring1")
+                for kb in range(TB):
+                    nc.tensor.transpose(
+                        live["e_key_ps"][:, kb * P : (kb + 1) * P], live["e_row"][:, kb * P : (kb + 1) * P], ident[:]
+                    )
+
+            def keys_out():
+                turned = live["e_key_ps"][:].rearrange("u (kb j) -> u kb j", kb=TB)
+                if qb % 2 == 0:
+                    nc.scalar.copy(e_key[:, b, :, qb * P : (qb + 1) * P], turned)
+                else:
+                    nc.vector.tensor_copy(e_key[:, b, :, qb * P : (qb + 1) * P], turned)
+
+            return [scores, maximum, exponential, turn_keys, keys_out]
+
+        def chain_stages(b):
+            seq = slice(b * T, (b + 1) * T)
+            live = {}
+
+            def turn(features_first, tokens_first):
+                turned_ps = bank(BF16, "turned_ps", "chain")
                 for kb in range(TB):
                     nc.tensor.transpose(
                         turned_ps[:, kb * P : (kb + 1) * P],
@@ -153,95 +223,120 @@ def tile_bertrewardmodel_b_kernel(
                     )
                 nc.scalar.copy(tokens_first[:, seq], turned_ps[:])
 
-        neg_max = held.tile([P, B * TB], F32, name="neg_max")
-        row_sum = held.tile([P, B * TB], F32, name="row_sum")
-        row_inv = held.tile([P, B * TB], F32, name="row_inv")
-        e_key = held.tile([P, B, TB, T], BF16, name="e_key")
-        at_t = held.tile([D, N], BF16, name="at_t")
-        hm = held.tile([D, N], BF16, name="hm")
-        x1_t = held.tile([D, N], F32, name="x1_t")
-        for b in range(B):
-            seq = slice(b * T, (b + 1) * T)
-            for qb in range(TB):
-                n = b * TB + qb
-                score = bank(F32, "score", "ring0")
-                nc.tensor.matmul(score[:], qr[:, n * P : (n + 1) * P], kr[:, seq], start=True, stop=True)
-                neg_score = ring.tile([P, T], F32, name="neg_score", bufs=4)
-                nc.vector.tensor_scalar(
-                    neg_score[:], score[:], -SCALE, None, op0=ALU.mult, op1=ALU.min, accum_out=neg_max[:, n : n + 1]
-                )
-                e_row = ring.tile([P, T], BF16, name="e_row", bufs=4)
-                nc.scalar.activation(
-                    e_row[:],
-                    neg_score[:],
-                    ACT.Exp,
-                    bias=neg_max[:, n : n + 1],
-                    scale=-1.0,
-                    accum_out=row_sum[:, n : n + 1],
-                )
-                e_key_ps = bank(BF16, "e_key_ps", "ring1")
+            def weighted_sum():
+                live["at_ps"] = bank(F32, "at_ps", "chain")
                 for kb in range(TB):
-                    nc.tensor.transpose(e_key_ps[:, kb * P : (kb + 1) * P], e_row[:, kb * P : (kb + 1) * P], ident[:])
-                turned = e_key_ps[:].rearrange("u (kb j) -> u kb j", kb=TB)
-                if qb % 2 == 0:
-                    nc.scalar.copy(e_key[:, b, :, qb * P : (qb + 1) * P], turned)
-                else:
-                    nc.vector.tensor_copy(e_key[:, b, :, qb * P : (qb + 1) * P], turned)
+                    nc.tensor.matmul(
+                        live["at_ps"][:],
+                        v_tok[:, b * T + kb * P : b * T + (kb + 1) * P],
+                        e_key[:, b, kb, :],
+                        start=(kb == 0),
+                        stop=(kb == TB - 1),
+                    )
 
-            at_ps = bank(F32, "at_ps", "sum")
-            for kb in range(TB):
-                nc.tensor.matmul(
-                    at_ps[:],
-                    v_tok[:, b * T + kb * P : b * T + (kb + 1) * P],
-                    e_key[:, b, kb, :],
-                    start=(kb == 0),
-                    stop=(kb == TB - 1),
-                )
-            nc.scalar.copy(at_t[:, seq], at_ps[:])
+            def weighted_sum_out():
+                nc.scalar.copy(at_t[:, seq], live["at_ps"][:])
 
-            proj_ps = bank(F32, "proj_ps", "norm")
-            for qb in range(TB):
-                n = b * TB + qb
-                nc.tensor.matmul(
-                    proj_ps[:, qb * P : (qb + 1) * P], at_t[:, n * P : (n + 1) * P], wo_t[:], start=True, stop=True
-                )
-            nc.vector.reciprocal(row_inv[:, b * TB : (b + 1) * TB], row_sum[:, b * TB : (b + 1) * TB])
-            x1_tok = ring.tile([P, T], F32, name="x1_tok", bufs=2)
-            stats = ring.tile([P, TB, BN_STATS], F32, name="stats")
-            mean_var = ring.tile([P, TB, BN_AGGR], F32, name="mean_var")
-            for qb in range(TB):
-                n = b * TB + qb
-                feats = slice(qb * P, (qb + 1) * P)
-                nc.vector.scalar_tensor_tensor(
-                    x1_tok[:, feats],
-                    proj_ps[:, feats],
-                    row_inv[:, n : n + 1],
-                    x_tok[:, n * P : (n + 1) * P],
-                    op0=ALU.mult,
-                    op1=ALU.add,
-                )
-                nc.vector.bn_stats(stats[:, qb, :], x1_tok[:, feats])
-                nc.vector.bn_aggr(mean_var[:, qb, :], stats[:, qb, :])
-            var_eps = ring.tile([P, TB, 1], F32, name="var_eps")
-            nc.vector.tensor_scalar(var_eps[:], mean_var[:, :, 1:2], EPS, None, op0=ALU.add)
-            rstd1 = ring.tile([P, TB, 1], F32, name="rstd1")
-            nc.gpsimd.tensor_tensor(rstd1[:], var_eps[:], minus_half[:], ALU.pow)
+            def project():
+                live["proj_ps"] = bank(F32, "proj_ps", "chain")
+                for qb in range(TB):
+                    n = b * TB + qb
+                    nc.tensor.matmul(
+                        live["proj_ps"][:, qb * P : (qb + 1) * P],
+                        at_t[:, n * P : (n + 1) * P],
+                        wo_t[:],
+                        start=True,
+                        stop=True,
+                    )
+                nc.vector.reciprocal(row_inv[:, b * TB : (b + 1) * TB], row_sum[:, b * TB : (b + 1) * TB])
+                live["x1_tok"] = ring.tile([P, T], F32, name="x1_tok", bufs=2)
+                live["stats"] = ring.tile([P, TB, BN_STATS], F32, name="stats")
+                live["mean_var"] = ring.tile([P, TB, BN_AGGR], F32, name="mean_var")
 
-            hm_ps = bank(F32, "hm_ps", "norm")
-            for qb in range(TB):
-                feats = slice(qb * P, (qb + 1) * P)
-                hm_tok = ring.tile([P, D], F32, name="hm_tok", bufs=4)
-                nc.vector.tensor_scalar(
-                    hm_tok[:], x1_tok[:, feats], mean_var[:, qb, 0:1], rstd1[:, qb, :], op0=ALU.subtract, op1=ALU.mult
-                )
-                nc.tensor.transpose(hm_ps[:, feats], hm_tok[:], ident_f[:])
-            nc.scalar.activation(hm[:, seq], hm_ps[:], ACT.Identity, scale=mlp_gain_t[:])
+            def residual_and_stats(blocks):
+                for qb in blocks:
+                    n = b * TB + qb
+                    feats = slice(qb * P, (qb + 1) * P)
+                    nc.vector.scalar_tensor_tensor(
+                        live["x1_tok"][:, feats],
+                        live["proj_ps"][:, feats],
+                        row_inv[:, n : n + 1],
+                        x_tok[:, n * P : (n + 1) * P],
+                        op0=ALU.mult,
+                        op1=ALU.add,
+                    )
+                    nc.vector.bn_stats(live["stats"][:, qb, :], live["x1_tok"][:, feats])
+                    nc.vector.bn_aggr(live["mean_var"][:, qb, :], live["stats"][:, qb, :])
 
-            x1_ps = bank(F32, "x1_ps", "norm")
-            for qb in range(TB):
-                feats = slice(qb * P, (qb + 1) * P)
-                nc.tensor.transpose(x1_ps[:, feats], x1_tok[:, feats], ident_f[:])
-            nc.scalar.copy(x1_t[:, seq], x1_ps[:])
+            def inverse_std():
+                var_eps = ring.tile([P, TB, 1], F32, name="var_eps")
+                nc.vector.tensor_scalar(var_eps[:], live["mean_var"][:, :, 1:2], EPS, None, op0=ALU.add)
+                live["rstd1"] = ring.tile([P, TB, 1], F32, name="rstd1")
+                nc.gpsimd.tensor_tensor(live["rstd1"][:], var_eps[:], minus_half[:], ALU.pow)
+
+            def normalise():
+                live["hm_ps"] = bank(F32, "hm_ps", "chain")
+                for qb in range(TB):
+                    feats = slice(qb * P, (qb + 1) * P)
+                    hm_tok = ring.tile([P, D], F32, name="hm_tok", bufs=4)
+                    nc.vector.tensor_scalar(
+                        hm_tok[:],
+                        live["x1_tok"][:, feats],
+                        live["mean_var"][:, qb, 0:1],
+                        live["rstd1"][:, qb, :],
+                        op0=ALU.subtract,
+                        op1=ALU.mult,
+                    )
+                    nc.tensor.transpose(live["hm_ps"][:, feats], hm_tok[:], ident_f[:])
+
+            def gain_and_round():
+                nc.scalar.activation(hm[:, seq], live["hm_ps"][:], ACT.Identity, scale=mlp_gain_t[:])
+
+            def turn_x1_back():
+                live["x1_ps"] = bank(F32, "x1_ps", "chain")
+                for qb in range(TB):
+                    feats = slice(qb * P, (qb + 1) * P)
+                    nc.tensor.transpose(live["x1_ps"][:, feats], live["x1_tok"][:, feats], ident_f[:])
+
+            def x1_out():
+                nc.scalar.copy(x1_t[:, seq], live["x1_ps"][:])
+
+            return [
+                lambda: turn(v_t, v_tok),
+                lambda: turn(x_t, x_tok),
+                weighted_sum,
+                weighted_sum_out,
+                project,
+                lambda: residual_and_stats((0, 1)),
+                lambda: residual_and_stats((2, 3)),
+                inverse_std,
+                normalise,
+                gain_and_round,
+                turn_x1_back,
+                x1_out,
+            ]
+
+        blocks = [softmax_stages(n) for n in range(B * TB)]
+        SOFTMAX_STAGES = 5
+        ROPE_LEAD = 6
+        rope_q = [rope_stages(b, wq_rot, q_cos, qr) for b in range(B)]
+        rope_k = [rope_stages(b, wk_rot, k_cos, kr) for b in range(B)]
+        ROPE_STAGES = 3
+        first_chain = chain_stages(0)
+        CHAIN_START = (TB - 1) + SOFTMAX_STAGES - 2
+        for step in range(-ROPE_LEAD, B * TB + SOFTMAX_STAGES - 1):
+            for stage in reversed(range(SOFTMAX_STAGES)):
+                n = step - stage
+                if 0 <= n < B * TB:
+                    blocks[n][stage]()
+            for b in range(B):
+                stage = step - (b * TB - ROPE_LEAD)
+                if 0 <= stage - 1 < ROPE_STAGES:
+                    rope_k[b][stage - 1]()
+                if 0 <= stage < ROPE_STAGES:
+                    rope_q[b][stage]()
+            if 0 <= step - CHAIN_START < len(first_chain):
+                first_chain[step - CHAIN_START]()
 
         wi_a_t = held.tile([D, I], BF16, name="wi_a_t")
         wi_gate_t = held.tile([D, I], BF16, name="wi_gate_t")
@@ -286,12 +381,16 @@ def tile_bertrewardmodel_b_kernel(
         for step in range(len(work) + LAG):
             if step < len(work):
                 b, a = work[step]
+                if a == 0 and b + 1 < B:
+                    stages = chain_stages(b + 1)
                 gelu_a = gelu_ahead
                 if step + 1 < len(work):
                     gelu_ahead = gelu_branch(work[step + 1][0], work[step + 1][1])
                 acts.append(gate_branch(b, a, gelu_a))
+                if b + 1 < B and a % 2 == 0 and a // 2 < len(stages):
+                    stages[a // 2]()
             if step >= LAG:
                 b, a = work[step - LAG]
                 if a == 0:
-                    out_banks.append(bank(F32, "out_ps", "sum" if b % 2 == 0 else "norm"))
+                    out_banks.append(bank(F32, "out_ps", "out"))
                 down(b, a, acts[step - LAG], out_banks[b])

@@ -94,19 +94,41 @@ def tile_bertrewardmodel_b_kernel(
             nc.vector.tensor_copy(rotated[:, D // 2 : D], plain[:, 0 : D // 2])
 
         window = held.tile([D, V], BF16, name="window")
-        for chunk in range(V // T):
+
+        def norm_stages(chunk):
             cols = slice(chunk * T, (chunk + 1) * T)
-            centred = bank(F32, "centred", "ring0")
-            nc.tensor.matmul(centred[:], centre[:], raw[:, cols], start=True, stop=True)
-            squares = ring.tile([D, T], F32, name="squares")
-            nc.scalar.activation(squares[:], centred[:], ACT.Square)
-            gained = ring.tile([D, T], F32, name="gained", bufs=4)
-            nc.vector.tensor_scalar(gained[:], centred[:], emb_gain_t[:], None, op0=ALU.mult)
-            variance = bank(F32, "variance", "ring1")
-            nc.tensor.matmul(variance[:], average[:], squares[:], start=True, stop=True)
-            rstd = ring.tile([D, T], F32, name="rstd")
-            nc.scalar.activation(rstd[:], variance[:], ACT.Abs_reciprocal_sqrt, bias=eps_t[:])
-            nc.vector.tensor_tensor(window[:, cols], gained[:], rstd[:], ALU.mult)
+            live = {}
+
+            def subtract_mean():
+                live["centred"] = bank(F32, "centred", "ring0")
+                nc.tensor.matmul(live["centred"][:], centre[:], raw[:, cols], start=True, stop=True)
+
+            def square_and_gain():
+                live["squares"] = ring.tile([D, T], F32, name="squares")
+                nc.scalar.activation(live["squares"][:], live["centred"][:], ACT.Square)
+                live["gained"] = ring.tile([D, T], F32, name="gained", bufs=5)
+                nc.vector.tensor_scalar(live["gained"][:], live["centred"][:], emb_gain_t[:], None, op0=ALU.mult)
+
+            def mean_of_squares():
+                live["variance"] = bank(F32, "variance", "ring1")
+                nc.tensor.matmul(live["variance"][:], average[:], live["squares"][:], start=True, stop=True)
+
+            def inverse_std():
+                live["rstd"] = ring.tile([D, T], F32, name="rstd")
+                nc.scalar.activation(live["rstd"][:], live["variance"][:], ACT.Abs_reciprocal_sqrt, bias=eps_t[:])
+
+            def scale_and_round():
+                nc.vector.tensor_tensor(window[:, cols], live["gained"][:], live["rstd"][:], ALU.mult)
+
+            return [subtract_mean, square_and_gain, mean_of_squares, inverse_std, scale_and_round]
+
+        chunks = [norm_stages(chunk) for chunk in range(V // T)]
+        NORM_STAGES = 5
+        for step in range(V // T + NORM_STAGES - 1):
+            for stage in range(NORM_STAGES):
+                chunk = step - stage
+                if 0 <= chunk < V // T:
+                    chunks[chunk][stage]()
 
         q_cos = held.tile([D, N], F32, name="q_cos")
         k_cos = held.tile([D, N], F32, name="k_cos")
@@ -312,9 +334,7 @@ def tile_bertrewardmodel_b_kernel(
                 inverse_std,
                 normalise,
                 gain_and_round,
-                turn_x1_back,
-                x1_out,
-            ]
+            ], [turn_x1_back, x1_out]
 
         blocks = [softmax_stages(n) for n in range(B * TB)]
         SOFTMAX_STAGES = 5
@@ -322,10 +342,10 @@ def tile_bertrewardmodel_b_kernel(
         rope_q = [rope_stages(b, wq_rot, q_cos, qr) for b in range(B)]
         rope_k = [rope_stages(b, wk_rot, k_cos, kr) for b in range(B)]
         ROPE_STAGES = 3
-        first_chain = chain_stages(0)
+        first_chain, x1_back = chain_stages(0)
         CHAIN_START = (TB - 1) + SOFTMAX_STAGES - 2
         for step in range(-ROPE_LEAD, B * TB + SOFTMAX_STAGES - 1):
-            for stage in reversed(range(SOFTMAX_STAGES)):
+            for stage in range(SOFTMAX_STAGES):
                 n = step - stage
                 if 0 <= n < B * TB:
                     blocks[n][stage]()
@@ -381,13 +401,16 @@ def tile_bertrewardmodel_b_kernel(
         for step in range(len(work) + LAG):
             if step < len(work):
                 b, a = work[step]
-                if a == 0 and b + 1 < B:
-                    stages = chain_stages(b + 1)
+                if a == 0:
+                    stages = x1_back
+                    if b + 1 < B:
+                        next_chain, x1_back = chain_stages(b + 1)
+                        stages = stages + next_chain
                 gelu_a = gelu_ahead
                 if step + 1 < len(work):
                     gelu_ahead = gelu_branch(work[step + 1][0], work[step + 1][1])
                 acts.append(gate_branch(b, a, gelu_a))
-                if b + 1 < B and a % 2 == 0 and a // 2 < len(stages):
+                if a % 2 == 0 and a // 2 < len(stages):
                     stages[a // 2]()
             if step >= LAG:
                 b, a = work[step - LAG]

@@ -165,7 +165,7 @@ def tile_bertrewardmodel_b_kernel(
         hm = held.tile([D, N], BF16, name="hm")
         x1_t = held.tile([D, N], F32, name="x1_t")
 
-        def rope_stages(b, rotated, cos_part, roped):
+        def rope_stages(b, rotated, cos_part, roped, adder):
             seq = slice(b * T, (b + 1) * T)
             live = {}
 
@@ -178,7 +178,7 @@ def tile_bertrewardmodel_b_kernel(
                 nc.vector.tensor_tensor(live["sin_part"][:], live["rot_ps"][:], sin_t[:], ALU.mult)
 
             def add_parts():
-                nc.gpsimd.tensor_tensor(roped[:, seq], cos_part[:, seq], live["sin_part"][:], ALU.add)
+                adder.tensor_tensor(roped[:, seq], cos_part[:, seq], live["sin_part"][:], ALU.add)
 
             return [rotate, times_sin, add_parts]
 
@@ -224,7 +224,7 @@ def tile_bertrewardmodel_b_kernel(
 
             def keys_out():
                 turned = live["e_key_ps"][:].rearrange("u (kb j) -> u kb j", kb=TB)
-                if qb % 2 == 0:
+                if qb % 2 == 0 and b < B - 1:
                     nc.scalar.copy(e_key[:, b, :, qb * P : (qb + 1) * P], turned)
                 else:
                     nc.vector.tensor_copy(e_key[:, b, :, qb * P : (qb + 1) * P], turned)
@@ -327,11 +327,13 @@ def tile_bertrewardmodel_b_kernel(
                 lambda: turn(v_t, v_tok),
                 lambda: turn(x_t, x_tok),
                 weighted_sum,
+                None,
                 weighted_sum_out,
                 project,
                 lambda: residual_and_stats((0, 1)),
                 lambda: residual_and_stats((2, 3)),
                 inverse_std,
+                None,
                 normalise,
                 gain_and_round,
             ], [turn_x1_back, x1_out]
@@ -339,8 +341,8 @@ def tile_bertrewardmodel_b_kernel(
         blocks = [softmax_stages(n) for n in range(B * TB)]
         SOFTMAX_STAGES = 5
         ROPE_LEAD = 6
-        rope_q = [rope_stages(b, wq_rot, q_cos, qr) for b in range(B)]
-        rope_k = [rope_stages(b, wk_rot, k_cos, kr) for b in range(B)]
+        rope_q = [rope_stages(b, wq_rot, q_cos, qr, nc.gpsimd) for b in range(B)]
+        rope_k = [rope_stages(b, wk_rot, k_cos, kr, nc.vector if b == 0 else nc.gpsimd) for b in range(B)]
         ROPE_STAGES = 3
         first_chain, x1_back = chain_stages(0)
         CHAIN_START = (TB - 1) + SOFTMAX_STAGES - 2
@@ -355,7 +357,7 @@ def tile_bertrewardmodel_b_kernel(
                     rope_k[b][stage - 1]()
                 if 0 <= stage < ROPE_STAGES:
                     rope_q[b][stage]()
-            if 0 <= step - CHAIN_START < len(first_chain):
+            if 0 <= step - CHAIN_START < len(first_chain) and first_chain[step - CHAIN_START]:
                 first_chain[step - CHAIN_START]()
 
         wi_a_t = held.tile([D, I], BF16, name="wi_a_t")
@@ -405,7 +407,7 @@ def tile_bertrewardmodel_b_kernel(
                     stages = x1_back
                     if b + 1 < B:
                         next_chain, x1_back = chain_stages(b + 1)
-                        stages = stages + next_chain
+                        stages = stages + [stage for stage in next_chain if stage]
                 gelu_a = gelu_ahead
                 if step + 1 < len(work):
                     gelu_ahead = gelu_branch(work[step + 1][0], work[step + 1][1])

@@ -24,7 +24,7 @@ BN_AGGR = 2
 EPS = 1e-5
 SCALE = 1.0 / math.sqrt(D)
 QUARTERS = 4
-LAG = 2
+LAG = 3
 
 FLOPS = 4 * 2 * D * D * N + 2 * 2 * D * T * T * B + 3 * 2 * D * I * N
 
@@ -347,6 +347,8 @@ def tile_bertrewardmodel_b_kernel(
         first_chain, x1_back = chain_stages(0)
         CHAIN_START = (TB - 1) + SOFTMAX_STAGES - 2
         for step in range(-ROPE_LEAD, B * TB + SOFTMAX_STAGES - 1):
+            if 0 <= step - CHAIN_START < len(first_chain) and first_chain[step - CHAIN_START]:
+                first_chain[step - CHAIN_START]()
             for stage in range(SOFTMAX_STAGES):
                 n = step - stage
                 if 0 <= n < B * TB:
@@ -357,8 +359,6 @@ def tile_bertrewardmodel_b_kernel(
                     rope_k[b][stage - 1]()
                 if 0 <= stage < ROPE_STAGES:
                     rope_q[b][stage]()
-            if 0 <= step - CHAIN_START < len(first_chain) and first_chain[step - CHAIN_START]:
-                first_chain[step - CHAIN_START]()
 
         wi_a_t = held.tile([D, I], BF16, name="wi_a_t")
         wi_gate_t = held.tile([D, I], BF16, name="wi_gate_t")

@@ -85,6 +85,8 @@ def tile_bertrewardmodel_b_kernel(
         nc.vector.memset(average[:], 1.0 / D)
         eps_t = held.tile([P, 1], F32, name="eps_t")
         nc.vector.memset(eps_t[:], EPS)
+        table_warm_up = held.tile([P, 1], F32, name="table_warm_up")
+        nc.scalar.activation(table_warm_up[:], eps_t[:], ACT.Abs_reciprocal_sqrt)
         minus_half = held.tile([P, TB, 1], F32, name="minus_half")
         nc.vector.memset(minus_half[:], -0.5)
         wq_rot = held.tile([D, D], BF16, name="wq_rot")
@@ -312,7 +314,10 @@ def tile_bertrewardmodel_b_kernel(
                     nc.tensor.transpose(live["hm_ps"][:, feats], hm_tok[:], ident_f[:])
 
             def gain_and_round():
-                nc.scalar.activation(hm[:, seq], live["hm_ps"][:], ACT.Identity, scale=mlp_gain_t[:])
+                if b == 0:
+                    nc.vector.tensor_scalar(hm[:, seq], live["hm_ps"][:], mlp_gain_t[:], None, op0=ALU.mult)
+                else:
+                    nc.scalar.activation(hm[:, seq], live["hm_ps"][:], ACT.Identity, scale=mlp_gain_t[:])
 
             def turn_x1_back():
                 live["x1_ps"] = bank(F32, "x1_ps", "chain")

import math

import concourse.mybir as mybir
from concourse.masks import make_identity

F32 = mybir.dt.float32
BF16 = mybir.dt.bfloat16
U16 = mybir.dt.uint16
ALU = mybir.AluOpType
ACT = mybir.ActivationFunctionType

P = 128
D = 128
V = 4096
B = 4
T = 512
N = B * T
TB = T // P
I = 4096
IB = I // P
PER_COLUMN = 16
BN_STATS = 6
BN_AGGR = 2
EPS = 1e-5
SCALE = 1.0 / math.sqrt(D)
QUARTERS = 4
LAG = 3

FLOPS = 4 * 2 * D * D * N + 2 * 2 * D * T * T * B + 3 * 2 * D * I * N


def tile_bertrewardmodel_b_kernel(
    tc, table, emb_gain, wq, wk, wv, cos, sin, wo, mlp_gain, wi_a, wi_gate, wmo, offs, out
):
    nc = tc.nc
    with (
        tc.tile_pool(name="held", bufs=1) as held,
        tc.tile_pool(name="ring", bufs=3) as ring,
        tc.psum_pool(name="psum", bufs=1) as psum,
    ):
        bank_bufs = {"ring0": 3, "ring1": 3, "chain": 1, "out": 1}

        def bank(dtype, name, tag):
            return psum.tile([P, T], dtype, name=name, tag=tag, bufs=bank_bufs[tag])

        emb_gain_t = held.tile([D, 1], F32, name="emb_gain_t")
        nc.sync.dma_start(emb_gain_t[:], emb_gain)
        raw = held.tile([D, V], BF16, name="raw")
        for chunk in range(V // T):
            cols = slice(chunk * T, (chunk + 1) * T)
            nc.sync.dma_start(raw[:, cols], table[:, cols])
        offsets = held.tile([P, N // PER_COLUMN], U16, name="offsets")
        nc.sync.dma_start(offsets[:], offs)
        wq_t = held.tile([D, D], BF16, name="wq_t")
        nc.sync.dma_start(wq_t[:], wq)
        wk_t = held.tile([D, D], BF16, name="wk_t")
        nc.sync.dma_start(wk_t[:], wk)
        wv_t = held.tile([D, D], BF16, name="wv_t")
        nc.sync.dma_start(wv_t[:], wv)
        cos_t = held.tile([D, T], F32, name="cos_t")
        nc.sync.dma_start(cos_t[:], cos)
        sin_t = held.tile([D, T], F32, name="sin_t")
        nc.sync.dma_start(sin_t[:], sin)
        wo_t = held.tile([D, D], BF16, name="wo_t")
        nc.sync.dma_start(wo_t[:], wo)
        mlp_gain_t = held.tile([D, 1], F32, name="mlp_gain_t")
        nc.sync.dma_start(mlp_gain_t[:], mlp_gain)
        wi_a_f = held.tile([D, I], F32, name="wi_a_f")
        wi_gate_f = held.tile([D, I], F32, name="wi_gate_f")
        wmo_f = held.tile([P, IB, D], F32, name="wmo_f")
        for quarter in range(QUARTERS):
            cols = slice(quarter * (I // QUARTERS), (quarter + 1) * (I // QUARTERS))
            hidden_blocks = slice(quarter * (IB // QUARTERS), (quarter + 1) * (IB // QUARTERS))
            nc.sync.dma_start(wi_a_f[:, cols], wi_a[:, cols])
            nc.sync.dma_start(wi_gate_f[:, cols], wi_gate[:, cols])
            nc.sync.dma_start(wmo_f[:, hidden_blocks, :], wmo[cols, :].rearrange("(a p) d -> p a d", p=P))

        ident = held.tile([P, P], BF16, name="ident")
        make_identity(nc, ident[:])
        ident_f = held.tile([P, P], F32, name="ident_f")
        make_identity(nc, ident_f[:])
        centre = held.tile([D, D], BF16, name="centre")
        nc.vector.tensor_scalar(centre[:], ident[:], -1.0 / D, None, op0=ALU.add)
        average = held.tile([D, D], F32, name="average")
        nc.vector.memset(average[:], 1.0 / D)
        eps_t = held.tile([P, 1], F32, name="eps_t")
        nc.vector.memset(eps_t[:], EPS)
        table_warm_up = held.tile([P, 1], F32, name="table_warm_up")
        nc.scalar.activation(table_warm_up[:], eps_t[:], ACT.Abs_reciprocal_sqrt)
        minus_half = held.tile([P, TB, 1], F32, name="minus_half")
        nc.vector.memset(minus_half[:], -0.5)
        wq_rot = held.tile([D, D], BF16, name="wq_rot")
        wk_rot = held.tile([D, D], BF16, name="wk_rot")
        for rotated, plain in ((wq_rot, wq_t), (wk_rot, wk_t)):
            nc.vector.tensor_scalar(rotated[:, 0 : D // 2], plain[:, D // 2 : D], -1.0, None, op0=ALU.mult)
            nc.vector.tensor_copy(rotated[:, D // 2 : D], plain[:, 0 : D // 2])

        window = held.tile([D, V], BF16, name="window")

        def norm_stages(chunk):
            cols = slice(chunk * T, (chunk + 1) * T)
            live = {}

            def subtract_mean():
                live["centred"] = bank(F32, "centred", "ring0")
                nc.tensor.matmul(live["centred"][:], centre[:], raw[:, cols], start=True, stop=True)

            def square_and_gain():
                live["squares"] = ring.tile([D, T], F32, name="squares")
                nc.scalar.activation(live["squares"][:], live["centred"][:], ACT.Square)
                live["gained"] = ring.tile([D, T], F32, name="gained", bufs=5)
                nc.vector.tensor_scalar(live["gained"][:], live["centred"][:], emb_gain_t[:], None, op0=ALU.mult)

            def mean_of_squares():
                live["variance"] = bank(F32, "variance", "ring1")
                nc.tensor.matmul(live["variance"][:], average[:], live["squares"][:], start=True, stop=True)

            def inverse_std():
                live["rstd"] = ring.tile([D, T], F32, name="rstd")
                nc.scalar.activation(live["rstd"][:], live["variance"][:], ACT.Abs_reciprocal_sqrt, bias=eps_t[:])

            def scale_and_round():
                nc.vector.tensor_tensor(window[:, cols], live["gained"][:], live["rstd"][:], ALU.mult)

            return [subtract_mean, square_and_gain, mean_of_squares, inverse_std, scale_and_round]

        chunks = [norm_stages(chunk) for chunk in range(V // T)]
        NORM_STAGES = 5
        for step in range(V // T + NORM_STAGES - 1):
            for stage in range(NORM_STAGES):
                chunk = step - stage
                if 0 <= chunk < V // T:
                    chunks[chunk][stage]()

        q_cos = held.tile([D, N], F32, name="q_cos")
        k_cos = held.tile([D, N], F32, name="k_cos")
        v_t = held.tile([D, N], BF16, name="v_t")
        x_t = held.tile([D, N], BF16, name="x_t")
        looked_up = [
            window[:].indirect(offsets[:, b * (T // PER_COLUMN) : (b + 1) * (T // PER_COLUMN)]) for b in range(B)
        ]
        for b in range(B):
            seq = slice(b * T, (b + 1) * T)
            q_ps = bank(F32, "q_ps", "ring0")
            nc.tensor.matmul(q_ps[:], wq_t[:], looked_up[b], start=True, stop=True)
            nc.vector.tensor_tensor(q_cos[:, seq], q_ps[:], cos_t[:], ALU.mult)
            k_ps = bank(F32, "k_ps", "ring1")
            nc.tensor.matmul(k_ps[:], wk_t[:], looked_up[b], start=True, stop=True)
            nc.vector.tensor_tensor(k_cos[:, seq], k_ps[:], cos_t[:], ALU.mult)
            v_ps = bank(F32, "v_ps", "ring0")
            nc.tensor.matmul(v_ps[:], wv_t[:], looked_up[b], start=True, stop=True)
            nc.scalar.copy(v_t[:, seq], v_ps[:])
        for b in range(B):
            x_ps = bank(F32, "x_ps", "ring1")
            nc.tensor.matmul(x_ps[:], ident[:], looked_up[b], start=True, stop=True)
            nc.scalar.copy(x_t[:, b * T : (b + 1) * T], x_ps[:])

        qr = held.tile([D, N], BF16, name="qr")
        kr = held.tile([D, N], BF16, name="kr")
        v_tok = held.tile([P, N], BF16, name="v_tok")
        x_tok = held.tile([P, N], BF16, name="x_tok")
        neg_max = held.tile([P, B * TB], F32, name="neg_max")
        row_sum = held.tile([P, B * TB], F32, name="row_sum")
        row_inv = held.tile([P, B * TB], F32, name="row_inv")
        e_key = held.tile([P, B, TB, T], BF16, name="e_key")
        at_t = held.tile([D, N], BF16, name="at_t")
        hm = held.tile([D, N], BF16, name="hm")
        x1_t = held.tile([D, N], F32, name="x1_t")

        def rope_stages(b, rotated, cos_part, roped, adder):
            seq = slice(b * T, (b + 1) * T)
            live = {}

            def rotate():
                live["rot_ps"] = bank(F32, "rot_ps", "ring1")
                nc.tensor.matmul(live["rot_ps"][:], rotated[:], x_t[:, seq], start=True, stop=True)

            def times_sin():
                live["sin_part"] = ring.tile([D, T], F32, name="sin_part")
                nc.vector.tensor_tensor(live["sin_part"][:], live["rot_ps"][:], sin_t[:], ALU.mult)

            def add_parts():
                adder.tensor_tensor(roped[:, seq], cos_part[:, seq], live["sin_part"][:], ALU.add)

            return [rotate, times_sin, add_parts]

        def softmax_stages(n):
            b, qb = divmod(n, TB)
            live = {}

            def scores():
                live["score"] = bank(F32, "score", "ring0")
                nc.tensor.matmul(
                    live["score"][:], qr[:, n * P : (n + 1) * P], kr[:, b * T : (b + 1) * T], start=True, stop=True
                )

            def maximum():
                live["neg_score"] = ring.tile([P, T], F32, name="neg_score", bufs=4)
                nc.vector.tensor_scalar(
                    live["neg_score"][:],
                    live["score"][:],
                    -SCALE,
                    None,
                    op0=ALU.mult,
                    op1=ALU.min,
                    accum_out=neg_max[:, n : n + 1],
                )

            def exponential():
                live["e_row"] = ring.tile([P, T], BF16, name="e_row", bufs=4)
                nc.scalar.activation(
                    live["e_row"][:],
                    live["neg_score"][:],
                    ACT.Exp,
                    bias=neg_max[:, n : n + 1],
                    scale=-1.0,
                    accum_out=row_sum[:, n : n + 1],
                )

            def turn_keys():
                live["e_key_ps"] = bank(BF16, "e_key_ps", "ring1")
                for kb in range(TB):
                    nc.tensor.transpose(
                        live["e_key_ps"][:, kb * P : (kb + 1) * P], live["e_row"][:, kb * P : (kb + 1) * P], ident[:]
                    )

            def keys_out():
                turned = live["e_key_ps"][:].rearrange("u (kb j) -> u kb j", kb=TB)
                if qb % 2 == 0 and b < B - 1:
                    nc.scalar.copy(e_key[:, b, :, qb * P : (qb + 1) * P], turned)
                else:
                    nc.vector.tensor_copy(e_key[:, b, :, qb * P : (qb + 1) * P], turned)

            return [scores, maximum, exponential, turn_keys, keys_out]

        def chain_stages(b):
            seq = slice(b * T, (b + 1) * T)
            live = {}

            def turn(features_first, tokens_first):
                turned_ps = bank(BF16, "turned_ps", "chain")
                for kb in range(TB):
                    nc.tensor.transpose(
                        turned_ps[:, kb * P : (kb + 1) * P],
                        features_first[:, b * T + kb * P : b * T + (kb + 1) * P],
                        ident[:],
                    )
                nc.scalar.copy(tokens_first[:, seq], turned_ps[:])

            def weighted_sum():
                live["at_ps"] = bank(F32, "at_ps", "chain")
                for kb in range(TB):
                    nc.tensor.matmul(
                        live["at_ps"][:],
                        v_tok[:, b * T + kb * P : b * T + (kb + 1) * P],
                        e_key[:, b, kb, :],
                        start=(kb == 0),
                        stop=(kb == TB - 1),
                    )

            def weighted_sum_out():
                nc.scalar.copy(at_t[:, seq], live["at_ps"][:])

            def project():
                live["proj_ps"] = bank(F32, "proj_ps", "chain")
                for qb in range(TB):
                    n = b * TB + qb
                    nc.tensor.matmul(
                        live["proj_ps"][:, qb * P : (qb + 1) * P],
                        at_t[:, n * P : (n + 1) * P],
                        wo_t[:],
                        start=True,
                        stop=True,
                    )
                nc.vector.reciprocal(row_inv[:, b * TB : (b + 1) * TB], row_sum[:, b * TB : (b + 1) * TB])
                live["x1_tok"] = ring.tile([P, T], F32, name="x1_tok", bufs=2)
                live["stats"] = ring.tile([P, TB, BN_STATS], F32, name="stats")
                live["mean_var"] = ring.tile([P, TB, BN_AGGR], F32, name="mean_var")

            def residual_and_stats(blocks):
                for qb in blocks:
                    n = b * TB + qb
                    feats = slice(qb * P, (qb + 1) * P)
                    nc.vector.scalar_tensor_tensor(
                        live["x1_tok"][:, feats],
                        live["proj_ps"][:, feats],
                        row_inv[:, n : n + 1],
                        x_tok[:, n * P : (n + 1) * P],
                        op0=ALU.mult,
                        op1=ALU.add,
                    )
                    nc.vector.bn_stats(live["stats"][:, qb, :], live["x1_tok"][:, feats])
                    nc.vector.bn_aggr(live["mean_var"][:, qb, :], live["stats"][:, qb, :])

            def inverse_std():
                var_eps = ring.tile([P, TB, 1], F32, name="var_eps")
                nc.vector.tensor_scalar(var_eps[:], live["mean_var"][:, :, 1:2], EPS, None, op0=ALU.add)
                live["rstd1"] = ring.tile([P, TB, 1], F32, name="rstd1")
                nc.gpsimd.tensor_tensor(live["rstd1"][:], var_eps[:], minus_half[:], ALU.pow)

            def normalise():
                live["hm_ps"] = bank(F32, "hm_ps", "chain")
                for qb in range(TB):
                    feats = slice(qb * P, (qb + 1) * P)
                    hm_tok = ring.tile([P, D], F32, name="hm_tok", bufs=4)
                    nc.vector.tensor_scalar(
                        hm_tok[:],
                        live["x1_tok"][:, feats],
                        live["mean_var"][:, qb, 0:1],
                        live["rstd1"][:, qb, :],
                        op0=ALU.subtract,
                        op1=ALU.mult,
                    )
                    nc.tensor.transpose(live["hm_ps"][:, feats], hm_tok[:], ident_f[:])

            def gain_and_round():
                if b == 0:
                    nc.vector.tensor_scalar(hm[:, seq], live["hm_ps"][:], mlp_gain_t[:], None, op0=ALU.mult)
                else:
                    nc.scalar.activation(hm[:, seq], live["hm_ps"][:], ACT.Identity, scale=mlp_gain_t[:])

            def turn_x1_back():
                live["x1_ps"] = bank(F32, "x1_ps", "chain")
                for qb in range(TB):
                    feats = slice(qb * P, (qb + 1) * P)
                    nc.tensor.transpose(live["x1_ps"][:, feats], live["x1_tok"][:, feats], ident_f[:])

            def x1_out():
                nc.scalar.copy(x1_t[:, seq], live["x1_ps"][:])

            return [
                lambda: turn(v_t, v_tok),
                lambda: turn(x_t, x_tok),
                weighted_sum,
                None,
                weighted_sum_out,
                project,
                lambda: residual_and_stats((0, 1)),
                lambda: residual_and_stats((2, 3)),
                inverse_std,
                None,
                normalise,
                gain_and_round,
            ], [turn_x1_back, x1_out]

        blocks = [softmax_stages(n) for n in range(B * TB)]
        SOFTMAX_STAGES = 5
        ROPE_LEAD = 6
        rope_q = [rope_stages(b, wq_rot, q_cos, qr, nc.gpsimd) for b in range(B)]
        rope_k = [rope_stages(b, wk_rot, k_cos, kr, nc.vector if b == 0 else nc.gpsimd) for b in range(B)]
        ROPE_STAGES = 3
        first_chain, x1_back = chain_stages(0)
        CHAIN_START = (TB - 1) + SOFTMAX_STAGES - 2
        for step in range(-ROPE_LEAD, B * TB + SOFTMAX_STAGES - 1):
            if 0 <= step - CHAIN_START < len(first_chain) and first_chain[step - CHAIN_START]:
                first_chain[step - CHAIN_START]()
            for stage in range(SOFTMAX_STAGES):
                n = step - stage
                if 0 <= n < B * TB:
                    blocks[n][stage]()
            for b in range(B):
                stage = step - (b * TB - ROPE_LEAD)
                if 0 <= stage - 1 < ROPE_STAGES:
                    rope_k[b][stage - 1]()
                if 0 <= stage < ROPE_STAGES:
                    rope_q[b][stage]()

        wi_a_t = held.tile([D, I], BF16, name="wi_a_t")
        wi_gate_t = held.tile([D, I], BF16, name="wi_gate_t")
        wmo_t = held.tile([P, IB, D], BF16, name="wmo_t")
        for part in range(I // T):
            cols = slice(part * T, (part + 1) * T)
            hidden_blocks = slice(part * TB, (part + 1) * TB)
            nc.gpsimd.tensor_scalar(wi_a_t[:, cols], wi_a_f[:, cols], 1.0, 0.0, op0=ALU.mult, op1=ALU.add)
            nc.gpsimd.tensor_scalar(wi_gate_t[:, cols], wi_gate_f[:, cols], 1.0, 0.0, op0=ALU.mult, op1=ALU.add)
            nc.gpsimd.tensor_scalar(
                wmo_t[:, hidden_blocks, :], wmo_f[:, hidden_blocks, :], 1.0, 0.0, op0=ALU.mult, op1=ALU.add
            )

        def gelu_branch(b, a):
            a_ps = bank(F32, "a_ps", "ring1")
            nc.tensor.matmul(a_ps[:], wi_a_t[:, a * P : (a + 1) * P], hm[:, b * T : (b + 1) * T], start=True, stop=True)
            gelu_a = ring.tile([P, T], F32, name="gelu_a", bufs=4)
            nc.scalar.activation(gelu_a[:], a_ps[:], ACT.Gelu)
            return gelu_a

        def gate_branch(b, a, gelu_a):
            c_ps = bank(F32, "c_ps", "ring0")
            nc.tensor.matmul(
                c_ps[:], wi_gate_t[:, a * P : (a + 1) * P], hm[:, b * T : (b + 1) * T], start=True, stop=True
            )
            act = ring.tile([P, T], BF16, name="act", bufs=LAG + 4)
            nc.vector.tensor_tensor(act[:], c_ps[:], gelu_a[:], ALU.mult)
            return act

        def down(b, a, act, out_ps):
            nc.tensor.matmul(out_ps[:], wmo_t[:, a, :], act[:], start=(a == 0), stop=(a == IB - 1))
            if a == IB - 1:
                seq = slice(b * T, (b + 1) * T)
                result = ring.tile([D, T], F32, name="result", bufs=2)
                nc.vector.tensor_tensor(result[:], out_ps[:], x1_t[:, seq], ALU.add)
                nc.sync.dma_start(out[:, seq], result[:])

        work = [(b, a) for b in range(B) for a in range(IB)]
        acts = []
        out_banks = []
        gelu_ahead = gelu_branch(0, 0)
        for step in range(len(work) + LAG):
            if step < len(work):
                b, a = work[step]
                if a == 0:
                    stages = x1_back
                    if b + 1 < B:
                        next_chain, x1_back = chain_stages(b + 1)
                        stages = stages + [stage for stage in next_chain if stage]
                gelu_a = gelu_ahead
                if step + 1 < len(work):
                    gelu_ahead = gelu_branch(work[step + 1][0], work[step + 1][1])
                acts.append(gate_branch(b, a, gelu_a))
                if a % 2 == 0 and a // 2 < len(stages):
                    stages[a // 2]()
            if step >= LAG:
                b, a = work[step - LAG]
                if a == 0:
                    out_banks.append(bank(F32, "out_ps", "out"))
                down(b, a, acts[step - LAG], out_banks[b])
